import numpy as np
import ml_dtypes


def mxq(x, axis, fmt="e4m3"):
    dtype, down = {"e4m3": (ml_dtypes.float8_e4m3fn, 7), "e5m2": (ml_dtypes.float8_e5m2, 14)}[fmt]
    v = np.moveaxis(np.asarray(x, np.float32).astype(ml_dtypes.bfloat16).astype(np.float64), axis, -1)
    blocks = v.reshape(v.shape[:-1] + (-1, 32))
    amax = np.abs(blocks).max(-1, keepdims=True)
    byte = np.maximum(np.where(amax > 0, np.frexp(amax)[1] - 1 + 127, 0) - down, 1)
    scale = np.exp2(byte - 127.0)
    codes = (blocks / scale).astype(np.float32).astype(dtype).astype(np.float64)
    return np.moveaxis((codes * scale).reshape(v.shape), -1, axis)


WIDE = False


def mx_kscale(k):
    if not WIDE:
        return np.ones(k)
    levels = np.array([10, -10, 5, -5, 0])
    if k % 512:
        return np.exp2(np.random.permutation(np.resize(levels, k // 32))).repeat(32)
    a = np.empty((k // 512, 16))
    for p in range(k // 512):
        a[p, :8] = np.random.permutation(np.resize(levels, 8))
        for g in range(8):
            far = levels[np.abs(levels - a[p, g]) >= 10]
            a[p, g + 8] = far[np.random.randint(len(far))]
    return np.exp2(a.ravel()).repeat(32)


BF16 = ml_dtypes.bfloat16


def bf(x):
    return np.asarray(x, np.float32).astype(BF16)


def f64(x):
    return np.asarray(x).astype(np.float64)


B, DIN, H1, H2, N, I, K, O = 1024, 2048, 1024, 512, 32, 16, 256, 16
NI = N * I
LN_EPS = 1e-5


def setup_inputs():
    s, t = mx_kscale(H1), mx_kscale(H2)
    return {"h1": bf(np.maximum(np.random.standard_normal((B, H1)), 0.0) * s),
            "W2": bf(np.random.standard_normal((H1, H2)) * 1.4 / np.sqrt(H1) / s[:, None] * t),
            "b2": bf(np.random.standard_normal(H2) * 0.2 * t),
            "Wp": bf(np.random.standard_normal((N, H2, I)) * 1.4 / np.sqrt(H2) / t[None, :, None]),
            "bp": bf(np.random.standard_normal((N, I)) * 0.2),
            "ln_g": bf(1.0 + 0.1 * np.random.standard_normal((N, I))),
            "ln_b": bf(0.1 * np.random.standard_normal((N, I)))}


def reference(h1, W2, b2, Wp, bp, ln_g, ln_b):
    x = np.maximum((mxq(f64(h1), 1, "e4m3") @ mxq(f64(W2), 0, "e4m3")) + f64(b2), 0.0)
    wpf = f64(Wp).transpose(1, 0, 2).reshape(H2, NI)
    p = (mxq(x, 1, "e4m3") @ mxq(wpf, 0, "e4m3")).reshape(B, N, I) + f64(bp)
    mu = p.mean(-1, keepdims=True)
    var = ((p - mu) ** 2).mean(-1, keepdims=True)
    return (p - mu) / np.sqrt(var + LN_EPS) * f64(ln_g) + f64(ln_b)

@@ -1,0 +1,253 @@
+from contextlib import ExitStack
+
+import concourse.mybir as mybir
+from concourse.masks import make_identity
+
+F32 = mybir.dt.float32
+BF16 = mybir.dt.bfloat16
+U32 = mybir.dt.uint32
+U8 = mybir.dt.uint8
+FP8X4 = mybir.dt.float8_e4m3fn_x4
+ACT = mybir.ActivationFunctionType
+ALU = mybir.AluOpType
+
+P = 128
+PACK = 4
+K_PASS = P * PACK
+
+B, H1, H2 = 1024, 1024, 512
+CAPS, CAP_DIM = 32, 16
+NI = CAPS * CAP_DIM
+LN_EPS = 1e-5
+
+PASSES_1 = H1 // K_PASS
+H2_TILES = H2 // P
+NI_TILES = NI // P
+CAPS_PER_TILE = P // CAP_DIM
+ROW_TILES = B // P
+LAST_ROW_TILE = ROW_TILES - 1
+W2_VECTOR_UNITS = 96
+
+FLOPS = 2 * B * H1 * H2 + 2 * B * H2 * NI
+
+
+def tile_capsulenetwork_pa_kernel(tc, h1, W2, b2, Wp, bp, ln_g, ln_b, out):
+    nc = tc.nc
+    with ExitStack() as ctx:
+        keep = ctx.enter_context(tc.tile_pool(name="keep", bufs=1))
+        work = ctx.enter_context(tc.tile_pool(name="work", bufs=3))
+        psum = ctx.enter_context(tc.psum_pool(name="psum", bufs=4))
+
+        w2_raw = keep.tile([P, PASSES_1, PACK, H2], BF16)
+        h1_raw = keep.tile([P, ROW_TILES, H1], BF16)
+        wp_raw = keep.tile([P, CAPS, PACK, CAP_DIM], BF16)
+
+        def load_w2_pass(g):
+            nc.sync.dma_start(
+                out=w2_raw[:, g],
+                in_=W2[g * K_PASS : (g + 1) * K_PASS, :].rearrange("(q t) w -> q t w", t=PACK),
+            )
+
+        def load_h1_tile(j):
+            nc.sync.dma_start(out=h1_raw[:, j, :], in_=h1[j * P : (j + 1) * P, :])
+
+        load_w2_pass(0)
+        load_h1_tile(0)
+        load_w2_pass(1)
+        for j in range(1, ROW_TILES):
+            load_h1_tile(j)
+        nc.sync.dma_start(
+            out=wp_raw[:].rearrange("p n t i -> p n (t i)"),
+            in_=Wp.rearrange("n (p t) i -> p n (t i)", t=PACK),
+        )
+        gain = keep.tile([P, NI], BF16)
+        nc.sync.dma_start(out=gain[:], in_=ln_g.rearrange("n i -> (n i)").partition_broadcast(P))
+        shift = keep.tile([P, NI], BF16)
+        nc.sync.dma_start(out=shift[:], in_=ln_b.rearrange("n i -> (n i)").partition_broadcast(P))
+
+        b2_bf = keep.tile([P, H2_TILES], BF16)
+        nc.scalar.dma_start(out=b2_bf[:], in_=b2.rearrange("(m t) -> m t", t=H2_TILES))
+        bp_rows = keep.tile([P, P], BF16)
+        nc.vector.memset(bp_rows[:], 0.0)
+        nc.scalar.dma_start(out=bp_rows[0:NI_TILES, :], in_=bp.rearrange("(r n) i -> r (n i)", r=NI_TILES))
+
+        eps = keep.tile([P, 1], F32)
+        nc.vector.memset(eps[:], LN_EPS)
+        first_rsqrt = keep.tile([P, 1], F32)
+        nc.scalar.activation(out=first_rsqrt[:], in_=eps[:], func=ACT.Abs_reciprocal_sqrt)
+
+        ident = keep.tile([P, P], F32)
+        make_identity(nc, ident[:])
+        in_capsule = keep.tile([P, CAPS_PER_TILE], F32)
+        nc.vector.tensor_reduce(
+            out=in_capsule[:],
+            in_=ident[:].rearrange("p (n i) -> p n i", i=CAP_DIM),
+            axis=mybir.AxisListType.X,
+            op=ALU.add,
+        )
+        centre = keep.tile([P, P], F32)
+        nc.vector.scalar_tensor_tensor(
+            out=centre[:].rearrange("p (n i) -> p n i", i=CAP_DIM),
+            in0=in_capsule[:].unsqueeze(2).to_broadcast([P, CAPS_PER_TILE, CAP_DIM]),
+            scalar=-1.0 / CAP_DIM,
+            in1=ident[:].rearrange("p (n i) -> p n i", i=CAP_DIM),
+            op0=ALU.mult,
+            op1=ALU.add,
+        )
+
+        b2_col = keep.tile([P, H2_TILES], F32)
+        nc.vector.tensor_copy(out=b2_col[:], in_=b2_bf[:])
+
+        w2_grouped = keep.tile([P, PASSES_1, H2, PACK], BF16, align_bytes=64)
+        w2_codes = keep.tile([P, PASSES_1, H2], U32, align_bytes=64)
+        w2_scales = keep.tile([P, PASSES_1, H2], U8, align_bytes=64)
+        for g in range(PASSES_1):
+            grouped = w2_grouped[:, g].rearrange("p (t m) j -> p t m j", t=H2_TILES)
+            raw = w2_raw[:, g].rearrange("p j (m t) -> p t m j", t=H2_TILES)
+            nc.vector.tensor_copy(out=grouped[:, :, 0:W2_VECTOR_UNITS, :], in_=raw[:, :, 0:W2_VECTOR_UNITS, :])
+            nc.scalar.copy(out=grouped[:, :, W2_VECTOR_UNITS:P, :], in_=raw[:, :, W2_VECTOR_UNITS:P, :])
+        for g in range(PASSES_1):
+            nc.vector.quantize_mx(
+                out=w2_codes[:, g, :].bitcast(FP8X4),
+                scales=w2_scales[:, g, :],
+                in_=w2_grouped[:, g].rearrange("p c j -> p (c j)"),
+            )
+
+        wp_grouped = keep.tile([P, CAPS, CAP_DIM, PACK], BF16, align_bytes=64)
+        wp_codes = keep.tile([P, NI], U32, align_bytes=64)
+        wp_scales = keep.tile([P, NI], U8, align_bytes=64)
+
+        def quantise_wp():
+            nc.vector.tensor_copy(out=wp_grouped[:], in_=wp_raw[:].rearrange("p n t i -> p n i t"))
+            nc.vector.quantize_mx(
+                out=wp_codes[:].bitcast(FP8X4),
+                scales=wp_scales[:],
+                in_=wp_grouped[:].rearrange("p n i t -> p (n i t)"),
+            )
+
+        h1_words = h1_raw[:].bitcast(F32)
+        h1_grouped = keep.tile([P, ROW_TILES, PASSES_1, P, PACK], BF16, align_bytes=64)
+        h1_grouped_words = h1_grouped[:].bitcast(F32)
+        h1_codes = keep.tile([P, ROW_TILES, PASSES_1, P], U32, align_bytes=64)
+        h1_scales = keep.tile([P, ROW_TILES, PASSES_1, P], U8, align_bytes=64)
+        x_tiles = keep.tile([P, H2_TILES, B], BF16)
+        x_grouped = keep.tile([P, B, PACK], BF16, align_bytes=64)
+        x_codes = keep.tile([P, B], U32, align_bytes=64)
+        x_scales = keep.tile([P, B], U8, align_bytes=64)
+        u_t = keep.tile([P, NI_TILES, B], F32)
+        out_tiles = out.rearrange("(j p) n i -> j p (n i)", p=P)
+
+        def quantise_h1(j):
+            turned = psum.tile([P, PASSES_1 * 2, P], F32, tag="plain")
+            for g in range(PASSES_1):
+                for u in range(2):
+                    nc.tensor.transpose(
+                        turned[:, 2 * g + u, :], h1_words[:, j, 256 * g + u : 256 * (g + 1) : 2], ident[:]
+                    )
+            nc.scalar.copy(out=h1_grouped_words[:, j], in_=turned[:].rearrange("p (g u) b -> p g b u", u=2))
+            nc.vector.quantize_mx(
+                out=h1_codes[:, j].rearrange("p g b -> p (g b)").bitcast(FP8X4),
+                scales=h1_scales[:, j].rearrange("p g b -> p (g b)"),
+                in_=h1_grouped[:, j].rearrange("p g b t -> p (g b t)"),
+            )
+
+        def first_product(j):
+            rows = slice(j * P, (j + 1) * P)
+            acc = psum.tile([P, H2_TILES, P], F32, tag="mx")
+            for t in range(H2_TILES):
+                units = slice(t * P, (t + 1) * P)
+                for g in range(PASSES_1):
+                    nc.tensor.matmul_mx(
+                        out=acc[:, t, :],
+                        lhsT=w2_codes[:, g, units].bitcast(FP8X4),
+                        lhsT_scale=w2_scales[:, g, units],
+                        rhs=h1_codes[:, j, g, :].bitcast(FP8X4),
+                        rhs_scale=h1_scales[:, j, g, :],
+                        start=(g == 0),
+                        stop=(g == PASSES_1 - 1),
+                    )
+            for t in range(H2_TILES):
+                nc.scalar.activation(
+                    out=x_tiles[:, t, rows], in_=acc[:, t, :], func=ACT.Relu, bias=b2_col[:, t : t + 1], scale=1.0
+                )
+            nc.vector.tensor_copy(
+                out=x_grouped[:, rows, :].rearrange("p (c i) t -> p c t i", i=4),
+                in_=x_tiles[:, :, rows].rearrange("p t (c i) -> p c t i", i=4),
+            )
+            nc.vector.quantize_mx(
+                out=x_codes[:, rows].bitcast(FP8X4),
+                scales=x_scales[:, rows],
+                in_=x_grouped[:, rows, :].rearrange("p b t -> p (b t)"),
+            )
+
+        def second_product(j):
+            rows = slice(j * P, (j + 1) * P)
+            acc_t = psum.tile([P, NI_TILES, P], F32, tag="mx")
+            for r in range(NI_TILES):
+                cols = slice(r * P, (r + 1) * P)
+                nc.tensor.matmul_mx(
+                    out=acc_t[:, r, :],
+                    lhsT=wp_codes[:, cols].bitcast(FP8X4),
+                    lhsT_scale=wp_scales[:, cols],
+                    rhs=x_codes[:, rows].bitcast(FP8X4),
+                    rhs_scale=x_scales[:, rows],
+                    start=True,
+                    stop=True,
+                )
+            for r in range(NI_TILES):
+                nc.scalar.activation(
+                    out=u_t[:, r, rows], in_=acc_t[:, r, :], func=ACT.Identity, bias=bp_col[:, r : r + 1], scale=1.0
+                )
+
+        def layer_norm(j):
+            rows = slice(j * P, (j + 1) * P)
+            centred = psum.tile([P, NI], F32, tag="plain")
+            for r in range(NI_TILES):
+                nc.tensor.matmul(
+                    out=centred[:, r * P : (r + 1) * P], lhsT=u_t[:, r, rows], rhs=centre[:], start=True, stop=True
+                )
+            squares = work.tile([P, NI], F32)
+            nc.scalar.activation(out=squares[:], in_=centred[:], func=ACT.Square)
+            sum_sq = work.tile([P, CAPS], F32)
+            nc.vector.tensor_reduce(
+                out=sum_sq[:],
+                in_=squares[:].rearrange("p (n i) -> p n i", i=CAP_DIM),
+                axis=mybir.AxisListType.X,
+                op=ALU.add,
+            )
+            rstd = work.tile([P, CAPS], F32)
+            nc.scalar.activation(
+                out=rstd[:], in_=sum_sq[:], func=ACT.Abs_reciprocal_sqrt, bias=eps[:, 0:1], scale=1.0 / CAP_DIM
+            )
+            factor = work.tile([P, NI], F32)
+            factor_engine = nc.vector if j == LAST_ROW_TILE else nc.gpsimd
+            factor_engine.tensor_tensor(
+                out=factor[:].rearrange("p (n i) -> p n i", i=CAP_DIM),
+                in0=gain[:].rearrange("p (n i) -> p n i", i=CAP_DIM),
+                in1=rstd[:].unsqueeze(2).to_broadcast([P, CAPS, CAP_DIM]),
+                op=ALU.mult,
+            )
+            scaled = work.tile([P, NI], F32)
+            nc.vector.tensor_tensor(out=scaled[:], in0=centred[:], in1=factor[:], op=ALU.mult)
+            result = work.tile([P, NI], F32)
+            nc.vector.tensor_tensor(out=result[:], in0=scaled[:], in1=shift[:], op=ALU.add)
+            nc.sync.dma_start(out=out_tiles[j], in_=result[:])
+
+        for j in range(ROW_TILES):
+            quantise_h1(j)
+        quantise_wp()
+        for j in range(ROW_TILES):
+            first_product(j)
+
+        bp_rows_f = keep.tile([P, P], F32)
+        nc.vector.tensor_copy(out=bp_rows_f[:], in_=bp_rows[:])
+        bp_ps = psum.tile([P, P], F32, tag="plain")
+        nc.tensor.transpose(bp_ps[:], bp_rows_f[:], ident[:])
+        bp_col = keep.tile([P, NI_TILES], F32)
+        nc.vector.tensor_copy(out=bp_col[:], in_=bp_ps[:, 0:NI_TILES])
+
+        second_product(0)
+        for j in range(ROW_TILES):
+            if j + 1 < ROW_TILES:
+                second_product(j + 1)
+            layer_norm(j)

@@ -95,9 +95,6 @@ def tile_capsulenetwork_pa_kernel(tc, h1, W2, b2, Wp, bp, ln_g, ln_b, out):
             op1=ALU.add,
         )
 
-        b2_col = keep.tile([P, H2_TILES], F32)
-        nc.vector.tensor_copy(out=b2_col[:], in_=b2_bf[:])
-
         w2_grouped = keep.tile([P, PASSES_1, H2, PACK], BF16, align_bytes=64)
         w2_codes = keep.tile([P, PASSES_1, H2], U32, align_bytes=64)
         w2_scales = keep.tile([P, PASSES_1, H2], U8, align_bytes=64)
@@ -168,7 +165,7 @@ def tile_capsulenetwork_pa_kernel(tc, h1, W2, b2, Wp, bp, ln_g, ln_b, out):
                     )
             for t in range(H2_TILES):
                 nc.scalar.activation(
-                    out=x_tiles[:, t, rows], in_=acc[:, t, :], func=ACT.Relu, bias=b2_col[:, t : t + 1], scale=1.0
+                    out=x_tiles[:, t, rows], in_=acc[:, t, :], func=ACT.Relu, bias=b2_bf[:, t : t + 1], scale=1.0
                 )
             nc.vector.tensor_copy(
                 out=x_grouped[:, rows, :].rearrange("p (c i) t -> p c t i", i=4),
@@ -240,11 +237,11 @@ def tile_capsulenetwork_pa_kernel(tc, h1, W2, b2, Wp, bp, ln_g, ln_b, out):
             first_product(j)
 
         bp_rows_f = keep.tile([P, P], F32)
-        nc.vector.tensor_copy(out=bp_rows_f[:], in_=bp_rows[:])
+        nc.gpsimd.tensor_copy(out=bp_rows_f[:], in_=bp_rows[:])
         bp_ps = psum.tile([P, P], F32, tag="plain")
         nc.tensor.transpose(bp_ps[:], bp_rows_f[:], ident[:])
         bp_col = keep.tile([P, NI_TILES], F32)
-        nc.vector.tensor_copy(out=bp_col[:], in_=bp_ps[:, 0:NI_TILES])
+        nc.scalar.copy(out=bp_col[:], in_=bp_ps[:, 0:NI_TILES])
 
         second_product(0)
         for j in range(ROW_TILES):

@@ -26,6 +26,7 @@ NI_TILES = NI // P
 CAPS_PER_TILE = P // CAP_DIM
 ROW_TILES = B // P
 LAST_ROW_TILE = ROW_TILES - 1
+WP_BEHIND_TILE = 3
 W2_VECTOR_UNITS = 96
 
 FLOPS = 2 * B * H1 * H2 + 2 * B * H2 * NI
@@ -36,7 +37,9 @@ def tile_capsulenetwork_pa_kernel(tc, h1, W2, b2, Wp, bp, ln_g, ln_b, out):
     with ExitStack() as ctx:
         keep = ctx.enter_context(tc.tile_pool(name="keep", bufs=1))
         work = ctx.enter_context(tc.tile_pool(name="work", bufs=3))
+        psum_mx = ctx.enter_context(tc.psum_pool(name="psum_mx", bufs=3))
         psum = ctx.enter_context(tc.psum_pool(name="psum", bufs=4))
+        psum_shift = ctx.enter_context(tc.psum_pool(name="psum_shift", bufs=1))
 
         w2_raw = keep.tile([P, PASSES_1, PACK, H2], BF16)
         h1_raw = keep.tile([P, ROW_TILES, H1], BF16)
@@ -56,19 +59,23 @@ def tile_capsulenetwork_pa_kernel(tc, h1, W2, b2, Wp, bp, ln_g, ln_b, out):
         load_w2_pass(1)
         for j in range(1, ROW_TILES):
             load_h1_tile(j)
-        nc.sync.dma_start(
-            out=wp_raw[:].rearrange("p n t i -> p n (t i)"),
-            in_=Wp.rearrange("n (p t) i -> p n (t i)", t=PACK),
-        )
+            if j == WP_BEHIND_TILE:
+                nc.sync.dma_start(
+                    out=wp_raw[:].rearrange("p n t i -> p n (t i)"),
+                    in_=Wp.rearrange("n (p t) i -> p n (t i)", t=PACK),
+                )
         gain = keep.tile([P, NI], BF16)
         nc.sync.dma_start(out=gain[:], in_=ln_g.rearrange("n i -> (n i)").partition_broadcast(P))
-        shift = keep.tile([P, NI], BF16)
-        nc.sync.dma_start(out=shift[:], in_=ln_b.rearrange("n i -> (n i)").partition_broadcast(P))
+        shift_row = keep.tile([P, NI], BF16)
+        nc.gpsimd.memset(shift_row[:], 0.0)
+        nc.sync.dma_start(out=shift_row[0:1, :], in_=ln_b.rearrange("(o n) i -> o (n i)", o=1))
+        ones = keep.tile([P, P], BF16)
+        nc.gpsimd.memset(ones[:], 1.0)
 
         b2_bf = keep.tile([P, H2_TILES], BF16)
         nc.scalar.dma_start(out=b2_bf[:], in_=b2.rearrange("(m t) -> m t", t=H2_TILES))
         bp_rows = keep.tile([P, P], BF16)
-        nc.vector.memset(bp_rows[:], 0.0)
+        nc.gpsimd.memset(bp_rows[:], 0.0)
         nc.scalar.dma_start(out=bp_rows[0:NI_TILES, :], in_=bp.rearrange("(r n) i -> r (n i)", r=NI_TILES))
 
         eps = keep.tile([P, 1], F32)
@@ -98,12 +105,13 @@ def tile_capsulenetwork_pa_kernel(tc, h1, W2, b2, Wp, bp, ln_g, ln_b, out):
         w2_grouped = keep.tile([P, PASSES_1, H2, PACK], BF16, align_bytes=64)
         w2_codes = keep.tile([P, PASSES_1, H2], U32, align_bytes=64)
         w2_scales = keep.tile([P, PASSES_1, H2], U8, align_bytes=64)
-        for g in range(PASSES_1):
+        def regroup_w2(g):
             grouped = w2_grouped[:, g].rearrange("p (t m) j -> p t m j", t=H2_TILES)
             raw = w2_raw[:, g].rearrange("p j (m t) -> p t m j", t=H2_TILES)
             nc.vector.tensor_copy(out=grouped[:, :, 0:W2_VECTOR_UNITS, :], in_=raw[:, :, 0:W2_VECTOR_UNITS, :])
             nc.scalar.copy(out=grouped[:, :, W2_VECTOR_UNITS:P, :], in_=raw[:, :, W2_VECTOR_UNITS:P, :])
-        for g in range(PASSES_1):
+
+        def quantise_w2(g):
             nc.vector.quantize_mx(
                 out=w2_codes[:, g, :].bitcast(FP8X4),
                 scales=w2_scales[:, g, :],
@@ -134,7 +142,7 @@ def tile_capsulenetwork_pa_kernel(tc, h1, W2, b2, Wp, bp, ln_g, ln_b, out):
         u_t = keep.tile([P, NI_TILES, B], F32)
         out_tiles = out.rearrange("(j p) n i -> j p (n i)", p=P)
 
-        def quantise_h1(j):
+        def turn_h1(j):
             turned = psum.tile([P, PASSES_1 * 2, P], F32, tag="plain")
             for g in range(PASSES_1):
                 for u in range(2):
@@ -142,6 +150,8 @@ def tile_capsulenetwork_pa_kernel(tc, h1, W2, b2, Wp, bp, ln_g, ln_b, out):
                         turned[:, 2 * g + u, :], h1_words[:, j, 256 * g + u : 256 * (g + 1) : 2], ident[:]
                     )
             nc.scalar.copy(out=h1_grouped_words[:, j], in_=turned[:].rearrange("p (g u) b -> p g b u", u=2))
+
+        def quantise_h1(j):
             nc.vector.quantize_mx(
                 out=h1_codes[:, j].rearrange("p g b -> p (g b)").bitcast(FP8X4),
                 scales=h1_scales[:, j].rearrange("p g b -> p (g b)"),
@@ -150,7 +160,7 @@ def tile_capsulenetwork_pa_kernel(tc, h1, W2, b2, Wp, bp, ln_g, ln_b, out):
 
         def first_product(j):
             rows = slice(j * P, (j + 1) * P)
-            acc = psum.tile([P, H2_TILES, P], F32, tag="mx")
+            acc = psum_mx.tile([P, H2_TILES, P], F32, tag="mx")
             for t in range(H2_TILES):
                 units = slice(t * P, (t + 1) * P)
                 for g in range(PASSES_1):
@@ -167,6 +177,9 @@ def tile_capsulenetwork_pa_kernel(tc, h1, W2, b2, Wp, bp, ln_g, ln_b, out):
                 nc.scalar.activation(
                     out=x_tiles[:, t, rows], in_=acc[:, t, :], func=ACT.Relu, bias=b2_bf[:, t : t + 1], scale=1.0
                 )
+
+        def quantise_x(j):
+            rows = slice(j * P, (j + 1) * P)
             nc.vector.tensor_copy(
                 out=x_grouped[:, rows, :].rearrange("p (c i) t -> p c t i", i=4),
                 in_=x_tiles[:, :, rows].rearrange("p t (c i) -> p c t i", i=4),
@@ -179,7 +192,7 @@ def tile_capsulenetwork_pa_kernel(tc, h1, W2, b2, Wp, bp, ln_g, ln_b, out):
 
         def second_product(j):
             rows = slice(j * P, (j + 1) * P)
-            acc_t = psum.tile([P, NI_TILES, P], F32, tag="mx")
+            acc_t = psum_mx.tile([P, NI_TILES, P], F32, tag="mx")
             for r in range(NI_TILES):
                 cols = slice(r * P, (r + 1) * P)
                 nc.tensor.matmul_mx(
@@ -196,7 +209,9 @@ def tile_capsulenetwork_pa_kernel(tc, h1, W2, b2, Wp, bp, ln_g, ln_b, out):
                     out=u_t[:, r, rows], in_=acc_t[:, r, :], func=ACT.Identity, bias=bp_col[:, r : r + 1], scale=1.0
                 )
 
-        def layer_norm(j):
+        centred_of, sum_sq_of, factor_of, scaled_of = {}, {}, {}, {}
+
+        def centre_u(j):
             rows = slice(j * P, (j + 1) * P)
             centred = psum.tile([P, NI], F32, tag="plain")
             for r in range(NI_TILES):
@@ -205,16 +220,23 @@ def tile_capsulenetwork_pa_kernel(tc, h1, W2, b2, Wp, bp, ln_g, ln_b, out):
                 )
             squares = work.tile([P, NI], F32)
             nc.scalar.activation(out=squares[:], in_=centred[:], func=ACT.Square)
+            centred_of[j] = centred
+            sum_sq_of[j] = squares
+
+        def sum_squares(j):
             sum_sq = work.tile([P, CAPS], F32)
             nc.vector.tensor_reduce(
                 out=sum_sq[:],
-                in_=squares[:].rearrange("p (n i) -> p n i", i=CAP_DIM),
+                in_=sum_sq_of[j][:].rearrange("p (n i) -> p n i", i=CAP_DIM),
                 axis=mybir.AxisListType.X,
                 op=ALU.add,
             )
+            sum_sq_of[j] = sum_sq
+
+        def make_factor(j):
             rstd = work.tile([P, CAPS], F32)
             nc.scalar.activation(
-                out=rstd[:], in_=sum_sq[:], func=ACT.Abs_reciprocal_sqrt, bias=eps[:, 0:1], scale=1.0 / CAP_DIM
+                out=rstd[:], in_=sum_sq_of[j][:], func=ACT.Abs_reciprocal_sqrt, bias=eps[:, 0:1], scale=1.0 / CAP_DIM
             )
             factor = work.tile([P, NI], F32)
             factor_engine = nc.vector if j == LAST_ROW_TILE else nc.gpsimd
@@ -224,27 +246,54 @@ def tile_capsulenetwork_pa_kernel(tc, h1, W2, b2, Wp, bp, ln_g, ln_b, out):
                 in1=rstd[:].unsqueeze(2).to_broadcast([P, CAPS, CAP_DIM]),
                 op=ALU.mult,
             )
+            factor_of[j] = factor
+
+        def scale_rows(j):
             scaled = work.tile([P, NI], F32)
-            nc.vector.tensor_tensor(out=scaled[:], in0=centred[:], in1=factor[:], op=ALU.mult)
+            nc.vector.tensor_tensor(out=scaled[:], in0=centred_of[j][:], in1=factor_of[j][:], op=ALU.mult)
+            scaled_of[j] = scaled
+
+        def shift_and_store(j):
             result = work.tile([P, NI], F32)
-            nc.vector.tensor_tensor(out=result[:], in0=scaled[:], in1=shift[:], op=ALU.add)
+            nc.vector.tensor_tensor(out=result[:], in0=scaled_of[j][:], in1=shift[:], op=ALU.add)
             nc.sync.dma_start(out=out_tiles[j], in_=result[:])
 
-        for j in range(ROW_TILES):
-            quantise_h1(j)
-        quantise_wp()
-        for j in range(ROW_TILES):
-            first_product(j)
-
         bp_rows_f = keep.tile([P, P], F32)
-        nc.gpsimd.tensor_copy(out=bp_rows_f[:], in_=bp_rows[:])
-        bp_ps = psum.tile([P, P], F32, tag="plain")
-        nc.tensor.transpose(bp_ps[:], bp_rows_f[:], ident[:])
         bp_col = keep.tile([P, NI_TILES], F32)
-        nc.scalar.copy(out=bp_col[:], in_=bp_ps[:, 0:NI_TILES])
 
-        second_product(0)
-        for j in range(ROW_TILES):
-            if j + 1 < ROW_TILES:
-                second_product(j + 1)
-            layer_norm(j)
+        shift = psum_shift.tile([P, NI], F32)
+
+        def turn_bp():
+            nc.tensor.matmul(out=shift[:], lhsT=ones[:], rhs=shift_row[:], start=True, stop=True)
+            nc.gpsimd.tensor_copy(out=bp_rows_f[:], in_=bp_rows[:])
+            bp_ps = psum.tile([P, P], F32, tag="plain")
+            nc.tensor.transpose(bp_ps[:], bp_rows_f[:], ident[:])
+            nc.scalar.copy(out=bp_col[:], in_=bp_ps[:, 0:NI_TILES])
+
+        lag = (
+            (turn_h1, 0),
+            (quantise_h1, 2),
+            (first_product, 3),
+            (quantise_x, 5),
+            (second_product, 6),
+            (centre_u, 8),
+            (sum_squares, 9),
+            (make_factor, 9),
+            (scale_rows, 11),
+            (shift_and_store, 12),
+        )
+        with tc.manual_schedule(
+            engines={mybir.EngineType.PE, mybir.EngineType.Activation, mybir.EngineType.DVE}
+        ):
+            regroup_w2(0)
+            turn_h1(0)
+            regroup_w2(1)
+            quantise_w2(0)
+            quantise_w2(1)
+            for step in range(1, ROW_TILES + lag[-1][1]):
+                if step == 6:
+                    quantise_wp()
+                    turn_bp()
+                for stage, behind in sorted(lag, key=lambda entry: -entry[1]):
+                    if 0 <= step - behind < ROW_TILES:
+                        stage(step - behind)

@@ -26,7 +26,6 @@ NI_TILES = NI // P
 CAPS_PER_TILE = P // CAP_DIM
 ROW_TILES = B // P
 LAST_ROW_TILE = ROW_TILES - 1
-WP_BEHIND_TILE = 3
 W2_VECTOR_UNITS = 96
 
 FLOPS = 2 * B * H1 * H2 + 2 * B * H2 * NI
@@ -59,11 +58,10 @@ def tile_capsulenetwork_pa_kernel(tc, h1, W2, b2, Wp, bp, ln_g, ln_b, out):
         load_w2_pass(1)
         for j in range(1, ROW_TILES):
             load_h1_tile(j)
-            if j == WP_BEHIND_TILE:
-                nc.sync.dma_start(
-                    out=wp_raw[:].rearrange("p n t i -> p n (t i)"),
-                    in_=Wp.rearrange("n (p t) i -> p n (t i)", t=PACK),
-                )
+        nc.sync.dma_start(
+            out=wp_raw[:].rearrange("p n t i -> p n (t i)"),
+            in_=Wp.rearrange("n (p t) i -> p n (t i)", t=PACK),
+        )
         gain = keep.tile([P, NI], BF16)
         nc.sync.dma_start(out=gain[:], in_=ln_g.rearrange("n i -> (n i)").partition_broadcast(P))
         shift_row = keep.tile([P, NI], BF16)
@@ -178,12 +176,15 @@ def tile_capsulenetwork_pa_kernel(tc, h1, W2, b2, Wp, bp, ln_g, ln_b, out):
                     out=x_tiles[:, t, rows], in_=acc[:, t, :], func=ACT.Relu, bias=b2_bf[:, t : t + 1], scale=1.0
                 )
 
-        def quantise_x(j):
+        def gather_x(j):
             rows = slice(j * P, (j + 1) * P)
             nc.vector.tensor_copy(
                 out=x_grouped[:, rows, :].rearrange("p (c i) t -> p c t i", i=4),
                 in_=x_tiles[:, :, rows].rearrange("p t (c i) -> p c t i", i=4),
             )
+
+        def quantise_x(j):
+            rows = slice(j * P, (j + 1) * P)
             nc.vector.quantize_mx(
                 out=x_codes[:, rows].bitcast(FP8X4),
                 scales=x_scales[:, rows],
@@ -270,30 +271,41 @@ def tile_capsulenetwork_pa_kernel(tc, h1, W2, b2, Wp, bp, ln_g, ln_b, out):
             nc.tensor.transpose(bp_ps[:], bp_rows_f[:], ident[:])
             nc.scalar.copy(out=bp_col[:], in_=bp_ps[:, 0:NI_TILES])
 
-        lag = (
-            (turn_h1, 0),
-            (quantise_h1, 2),
-            (first_product, 3),
-            (quantise_x, 5),
-            (second_product, 6),
-            (centre_u, 8),
-            (sum_squares, 9),
-            (make_factor, 9),
-            (scale_rows, 11),
-            (shift_and_store, 12),
-        )
-        with tc.manual_schedule(
-            engines={mybir.EngineType.PE, mybir.EngineType.Activation, mybir.EngineType.DVE}
-        ):
+        def pipeline(stages):
+            for step in range(ROW_TILES + stages[0][1]):
+                for stage, lag in stages:
+                    if 0 <= step - lag < ROW_TILES:
+                        stage(step - lag)
+
+        with tc.manual_schedule(engines={mybir.EngineType.PE, mybir.EngineType.Activation, mybir.EngineType.DVE}):
             regroup_w2(0)
             turn_h1(0)
             regroup_w2(1)
             quantise_w2(0)
             quantise_w2(1)
-            for step in range(1, ROW_TILES + lag[-1][1]):
-                if step == 6:
+            for j in range(1, ROW_TILES):
+                turn_h1(j)
+                quantise_h1(j - 1)
+            quantise_h1(LAST_ROW_TILE)
+            for j in range(ROW_TILES):
+                first_product(j)
+                if j >= 1:
+                    gather_x(j - 1)
+                if j >= 2:
+                    quantise_x(j - 2)
+                if j == ROW_TILES // 2:
                     quantise_wp()
-                    turn_bp()
-                for stage, behind in sorted(lag, key=lambda entry: -entry[1]):
-                    if 0 <= step - behind < ROW_TILES:
-                        stage(step - behind)
+            gather_x(LAST_ROW_TILE)
+            quantise_x(LAST_ROW_TILE - 1)
+            quantise_x(LAST_ROW_TILE)
+            turn_bp()
+            pipeline(
+                (
+                    (shift_and_store, 6),
+                    (scale_rows, 5),
+                    (sum_squares, 3),
+                    (make_factor, 3),
+                    (centre_u, 2),
+                    (second_product, 0),
+                )
+            )

@@ -240,8 +240,7 @@ def tile_capsulenetwork_pa_kernel(tc, h1, W2, b2, Wp, bp, ln_g, ln_b, out):
                 out=rstd[:], in_=sum_sq_of[j][:], func=ACT.Abs_reciprocal_sqrt, bias=eps[:, 0:1], scale=1.0 / CAP_DIM
             )
             factor = work.tile([P, NI], F32)
-            factor_engine = nc.vector if j == LAST_ROW_TILE else nc.gpsimd
-            factor_engine.tensor_tensor(
+            nc.gpsimd.tensor_tensor(
                 out=factor[:].rearrange("p (n i) -> p n i", i=CAP_DIM),
                 in0=gain[:].rearrange("p (n i) -> p n i", i=CAP_DIM),
                 in1=rstd[:].unsqueeze(2).to_broadcast([P, CAPS, CAP_DIM]),
@@ -293,7 +292,7 @@ def tile_capsulenetwork_pa_kernel(tc, h1, W2, b2, Wp, bp, ln_g, ln_b, out):
                     gather_x(j - 1)
                 if j >= 2:
                     quantise_x(j - 2)
-                if j == ROW_TILES // 2:
+                if j == ROW_TILES // 2 - 1:
                     quantise_wp()
             gather_x(LAST_ROW_TILE)
             quantise_x(LAST_ROW_TILE - 1)
@@ -303,9 +302,9 @@ def tile_capsulenetwork_pa_kernel(tc, h1, W2, b2, Wp, bp, ln_g, ln_b, out):
                 (
                     (shift_and_store, 6),
                     (scale_rows, 5),
+                    (make_factor, 4),
+                    (centre_u, 3),
                     (sum_squares, 3),
-                    (make_factor, 3),
-                    (centre_u, 2),
                     (second_product, 0),
                 )
             )

@@ -25,7 +25,7 @@ H2_TILES = H2 // P
 NI_TILES = NI // P
 CAPS_PER_TILE = P // CAP_DIM
 ROW_TILES = B // P
-LAST_ROW_TILE = ROW_TILES - 1
+EARLY_TILES = 6
 W2_VECTOR_UNITS = 96
 
 FLOPS = 2 * B * H1 * H2 + 2 * B * H2 * NI
@@ -56,12 +56,14 @@ def tile_capsulenetwork_pa_kernel(tc, h1, W2, b2, Wp, bp, ln_g, ln_b, out):
         load_w2_pass(0)
         load_h1_tile(0)
         load_w2_pass(1)
-        for j in range(1, ROW_TILES):
+        for j in range(1, EARLY_TILES):
             load_h1_tile(j)
         nc.sync.dma_start(
             out=wp_raw[:].rearrange("p n t i -> p n (t i)"),
             in_=Wp.rearrange("n (p t) i -> p n (t i)", t=PACK),
         )
+        for j in range(EARLY_TILES, ROW_TILES):
+            load_h1_tile(j)
         gain = keep.tile([P, NI], BF16)
         nc.sync.dma_start(out=gain[:], in_=ln_g.rearrange("n i -> (n i)").partition_broadcast(P))
         shift_row = keep.tile([P, NI], BF16)
@@ -270,41 +272,43 @@ def tile_capsulenetwork_pa_kernel(tc, h1, W2, b2, Wp, bp, ln_g, ln_b, out):
             nc.tensor.transpose(bp_ps[:], bp_rows_f[:], ident[:])
             nc.scalar.copy(out=bp_col[:], in_=bp_ps[:, 0:NI_TILES])
 
-        def pipeline(stages):
-            for step in range(ROW_TILES + stages[0][1]):
-                for stage, lag in stages:
-                    if 0 <= step - lag < ROW_TILES:
-                        stage(step - lag)
-
         with tc.manual_schedule(engines={mybir.EngineType.PE, mybir.EngineType.Activation, mybir.EngineType.DVE}):
             regroup_w2(0)
             turn_h1(0)
             regroup_w2(1)
             quantise_w2(0)
             quantise_w2(1)
-            for j in range(1, ROW_TILES):
+            for j in range(1, EARLY_TILES):
                 turn_h1(j)
                 quantise_h1(j - 1)
-            quantise_h1(LAST_ROW_TILE)
-            for j in range(ROW_TILES):
+            quantise_h1(EARLY_TILES - 1)
+            for j in range(EARLY_TILES):
                 first_product(j)
+                if j == 1:
+                    quantise_wp()
                 if j >= 1:
                     gather_x(j - 1)
                 if j >= 2:
                     quantise_x(j - 2)
-                if j == ROW_TILES // 2 - 1:
-                    quantise_wp()
-            gather_x(LAST_ROW_TILE)
-            quantise_x(LAST_ROW_TILE - 1)
-            quantise_x(LAST_ROW_TILE)
+            gather_x(EARLY_TILES - 1)
+            quantise_x(EARLY_TILES - 2)
+            quantise_x(EARLY_TILES - 1)
             turn_bp()
-            pipeline(
-                (
-                    (shift_and_store, 6),
-                    (scale_rows, 5),
-                    (make_factor, 4),
-                    (centre_u, 3),
-                    (sum_squares, 3),
-                    (second_product, 0),
-                )
-            )
+            every = range(ROW_TILES)
+            late = range(EARLY_TILES, ROW_TILES)
+            for step in range(ROW_TILES + 5):
+                for stage, lag, tiles in (
+                    (centre_u, 2, every),
+                    (make_factor, 3, every),
+                    (first_product, -3, late),
+                    (shift_and_store, 5, every),
+                    (quantise_x, -1, late),
+                    (gather_x, -2, late),
+                    (scale_rows, 4, every),
+                    (quantise_h1, -5, late),
+                    (sum_squares, 2, every),
+                    (turn_h1, -6, late),
+                    (second_product, 0, every),
+                ):
+                    if step - lag in tiles:
+                        stage(step - lag)

@@ -122,8 +122,10 @@ def tile_capsulenetwork_pa_kernel(tc, h1, W2, b2, Wp, bp, ln_g, ln_b, out):
         wp_codes = keep.tile([P, NI], U32, align_bytes=64)
         wp_scales = keep.tile([P, NI], U8, align_bytes=64)
 
-        def quantise_wp():
+        def regroup_wp():
             nc.vector.tensor_copy(out=wp_grouped[:], in_=wp_raw[:].rearrange("p n t i -> p n i t"))
+
+        def quantise_wp():
             nc.vector.quantize_mx(
                 out=wp_codes[:].bitcast(FP8X4),
                 scales=wp_scales[:],
@@ -142,6 +144,8 @@ def tile_capsulenetwork_pa_kernel(tc, h1, W2, b2, Wp, bp, ln_g, ln_b, out):
         u_t = keep.tile([P, NI_TILES, B], F32)
         out_tiles = out.rearrange("(j p) n i -> j p (n i)", p=P)
 
+        turned_of = {}
+
         def turn_h1(j):
             turned = psum.tile([P, PASSES_1 * 2, P], F32, tag="plain")
             for g in range(PASSES_1):
@@ -149,7 +153,10 @@ def tile_capsulenetwork_pa_kernel(tc, h1, W2, b2, Wp, bp, ln_g, ln_b, out):
                     nc.tensor.transpose(
                         turned[:, 2 * g + u, :], h1_words[:, j, 256 * g + u : 256 * (g + 1) : 2], ident[:]
                     )
-            nc.scalar.copy(out=h1_grouped_words[:, j], in_=turned[:].rearrange("p (g u) b -> p g b u", u=2))
+            turned_of[j] = turned
+
+        def group_h1(j):
+            nc.scalar.copy(out=h1_grouped_words[:, j], in_=turned_of[j][:].rearrange("p (g u) b -> p g b u", u=2))
 
         def quantise_h1(j):
             nc.vector.quantize_mx(
@@ -214,6 +221,11 @@ def tile_capsulenetwork_pa_kernel(tc, h1, W2, b2, Wp, bp, ln_g, ln_b, out):
 
         centred_of, sum_sq_of, factor_of, scaled_of = {}, {}, {}, {}
 
+        def capsule_parts(j):
+            if j == ROW_TILES - 1:
+                return (slice(0, CAPS // 2), slice(CAPS // 2, CAPS))
+            return (slice(0, CAPS),)
+
         def centre_u(j):
             rows = slice(j * P, (j + 1) * P)
             centred = psum.tile([P, NI], F32, tag="plain")
@@ -242,23 +254,31 @@ def tile_capsulenetwork_pa_kernel(tc, h1, W2, b2, Wp, bp, ln_g, ln_b, out):
                 out=rstd[:], in_=sum_sq_of[j][:], func=ACT.Abs_reciprocal_sqrt, bias=eps[:, 0:1], scale=1.0 / CAP_DIM
             )
             factor = work.tile([P, NI], F32)
-            nc.gpsimd.tensor_tensor(
-                out=factor[:].rearrange("p (n i) -> p n i", i=CAP_DIM),
-                in0=gain[:].rearrange("p (n i) -> p n i", i=CAP_DIM),
-                in1=rstd[:].unsqueeze(2).to_broadcast([P, CAPS, CAP_DIM]),
-                op=ALU.mult,
-            )
+            for caps in capsule_parts(j):
+                cols = slice(caps.start * CAP_DIM, caps.stop * CAP_DIM)
+                nc.gpsimd.tensor_tensor(
+                    out=factor[:, cols].rearrange("p (n i) -> p n i", i=CAP_DIM),
+                    in0=gain[:, cols].rearrange("p (n i) -> p n i", i=CAP_DIM),
+                    in1=rstd[:, caps].unsqueeze(2).to_broadcast([P, caps.stop - caps.start, CAP_DIM]),
+                    op=ALU.mult,
+                )
             factor_of[j] = factor
 
         def scale_rows(j):
             scaled = work.tile([P, NI], F32)
-            nc.vector.tensor_tensor(out=scaled[:], in0=centred_of[j][:], in1=factor_of[j][:], op=ALU.mult)
+            for caps in capsule_parts(j):
+                cols = slice(caps.start * CAP_DIM, caps.stop * CAP_DIM)
+                nc.vector.tensor_tensor(
+                    out=scaled[:, cols], in0=centred_of[j][:, cols], in1=factor_of[j][:, cols], op=ALU.mult
+                )
             scaled_of[j] = scaled
 
         def shift_and_store(j):
             result = work.tile([P, NI], F32)
-            nc.vector.tensor_tensor(out=result[:], in0=scaled_of[j][:], in1=shift[:], op=ALU.add)
-            nc.sync.dma_start(out=out_tiles[j], in_=result[:])
+            for caps in capsule_parts(j):
+                cols = slice(caps.start * CAP_DIM, caps.stop * CAP_DIM)
+                nc.vector.tensor_tensor(out=result[:, cols], in0=scaled_of[j][:, cols], in1=shift[:, cols], op=ALU.add)
+                nc.sync.dma_start(out=out_tiles[j][:, cols], in_=result[:, cols])
 
         bp_rows_f = keep.tile([P, P], F32)
         bp_col = keep.tile([P, NI_TILES], F32)
@@ -275,20 +295,25 @@ def tile_capsulenetwork_pa_kernel(tc, h1, W2, b2, Wp, bp, ln_g, ln_b, out):
         with tc.manual_schedule(engines={mybir.EngineType.PE, mybir.EngineType.Activation, mybir.EngineType.DVE}):
             regroup_w2(0)
             turn_h1(0)
+            group_h1(0)
             regroup_w2(1)
             quantise_w2(0)
             quantise_w2(1)
             for j in range(1, EARLY_TILES):
                 turn_h1(j)
+                group_h1(j)
                 quantise_h1(j - 1)
             quantise_h1(EARLY_TILES - 1)
             for j in range(EARLY_TILES):
                 first_product(j)
                 if j == 1:
+                    regroup_wp()
+                    gather_x(0)
                     quantise_wp()
-                if j >= 1:
-                    gather_x(j - 1)
+                    quantise_x(0)
                 if j >= 2:
+                    gather_x(j - 1)
+                if j >= 3:
                     quantise_x(j - 2)
             gather_x(EARLY_TILES - 1)
             quantise_x(EARLY_TILES - 2)
@@ -305,10 +330,11 @@ def tile_capsulenetwork_pa_kernel(tc, h1, W2, b2, Wp, bp, ln_g, ln_b, out):
                     (quantise_x, -1, late),
                     (gather_x, -2, late),
                     (scale_rows, 4, every),
-                    (quantise_h1, -5, late),
                     (sum_squares, 2, every),
+                    (quantise_h1, -5, late),
                     (turn_h1, -6, late),
                     (second_product, 0, every),
+                    (group_h1, -6, late),
                 ):
                     if step - lag in tiles:
                         stage(step - lag)

@@ -286,11 +286,13 @@ def tile_capsulenetwork_pa_kernel(tc, h1, W2, b2, Wp, bp, ln_g, ln_b, out):
         shift = psum_shift.tile([P, NI], F32)
 
         def turn_bp():
-            nc.tensor.matmul(out=shift[:], lhsT=ones[:], rhs=shift_row[:], start=True, stop=True)
             nc.gpsimd.tensor_copy(out=bp_rows_f[:], in_=bp_rows[:])
             bp_ps = psum.tile([P, P], F32, tag="plain")
             nc.tensor.transpose(bp_ps[:], bp_rows_f[:], ident[:])
             nc.scalar.copy(out=bp_col[:], in_=bp_ps[:, 0:NI_TILES])
+
+        def spread_shift():
+            nc.tensor.matmul(out=shift[:], lhsT=ones[:], rhs=shift_row[:], start=True, stop=True)
 
         with tc.manual_schedule(engines={mybir.EngineType.PE, mybir.EngineType.Activation, mybir.EngineType.DVE}):
             regroup_w2(0)
@@ -306,6 +308,8 @@ def tile_capsulenetwork_pa_kernel(tc, h1, W2, b2, Wp, bp, ln_g, ln_b, out):
             quantise_h1(EARLY_TILES - 1)
             for j in range(EARLY_TILES):
                 first_product(j)
+                if j == 2:
+                    turn_bp()
                 if j == 1:
                     regroup_wp()
                     gather_x(0)
@@ -318,10 +322,11 @@ def tile_capsulenetwork_pa_kernel(tc, h1, W2, b2, Wp, bp, ln_g, ln_b, out):
             gather_x(EARLY_TILES - 1)
             quantise_x(EARLY_TILES - 2)
             quantise_x(EARLY_TILES - 1)
-            turn_bp()
             every = range(ROW_TILES)
             late = range(EARLY_TILES, ROW_TILES)
             for step in range(ROW_TILES + 5):
+                if step == 3:
+                    spread_shift()
                 for stage, lag, tiles in (
                     (centre_u, 2, every),
                     (make_factor, 3, every),

from contextlib import ExitStack

import concourse.mybir as mybir
from concourse.masks import make_identity

F32 = mybir.dt.float32
BF16 = mybir.dt.bfloat16
U32 = mybir.dt.uint32
U8 = mybir.dt.uint8
FP8X4 = mybir.dt.float8_e4m3fn_x4
ACT = mybir.ActivationFunctionType
ALU = mybir.AluOpType

P = 128
PACK = 4
K_PASS = P * PACK

B, H1, H2 = 1024, 1024, 512
CAPS, CAP_DIM = 32, 16
NI = CAPS * CAP_DIM
LN_EPS = 1e-5

PASSES_1 = H1 // K_PASS
H2_TILES = H2 // P
NI_TILES = NI // P
CAPS_PER_TILE = P // CAP_DIM
ROW_TILES = B // P
EARLY_TILES = 6
W2_VECTOR_UNITS = 96

FLOPS = 2 * B * H1 * H2 + 2 * B * H2 * NI


def tile_capsulenetwork_pa_kernel(tc, h1, W2, b2, Wp, bp, ln_g, ln_b, out):
    nc = tc.nc
    with ExitStack() as ctx:
        keep = ctx.enter_context(tc.tile_pool(name="keep", bufs=1))
        work = ctx.enter_context(tc.tile_pool(name="work", bufs=3))
        psum_mx = ctx.enter_context(tc.psum_pool(name="psum_mx", bufs=3))
        psum = ctx.enter_context(tc.psum_pool(name="psum", bufs=4))
        psum_shift = ctx.enter_context(tc.psum_pool(name="psum_shift", bufs=1))

        w2_raw = keep.tile([P, PASSES_1, PACK, H2], BF16)
        h1_raw = keep.tile([P, ROW_TILES, H1], BF16)
        wp_raw = keep.tile([P, CAPS, PACK, CAP_DIM], BF16)

        def load_w2_pass(g):
            nc.sync.dma_start(
                out=w2_raw[:, g],
                in_=W2[g * K_PASS : (g + 1) * K_PASS, :].rearrange("(q t) w -> q t w", t=PACK),
            )

        def load_h1_tile(j):
            nc.sync.dma_start(out=h1_raw[:, j, :], in_=h1[j * P : (j + 1) * P, :])

        load_w2_pass(0)
        load_h1_tile(0)
        load_w2_pass(1)
        for j in range(1, EARLY_TILES):
            load_h1_tile(j)
        nc.sync.dma_start(
            out=wp_raw[:].rearrange("p n t i -> p n (t i)"),
            in_=Wp.rearrange("n (p t) i -> p n (t i)", t=PACK),
        )
        for j in range(EARLY_TILES, ROW_TILES):
            load_h1_tile(j)
        gain = keep.tile([P, NI], BF16)
        nc.sync.dma_start(out=gain[:], in_=ln_g.rearrange("n i -> (n i)").partition_broadcast(P))
        shift_row = keep.tile([P, NI], BF16)
        nc.gpsimd.memset(shift_row[:], 0.0)
        nc.sync.dma_start(out=shift_row[0:1, :], in_=ln_b.rearrange("(o n) i -> o (n i)", o=1))
        ones = keep.tile([P, P], BF16)
        nc.gpsimd.memset(ones[:], 1.0)

        b2_bf = keep.tile([P, H2_TILES], BF16)
        nc.scalar.dma_start(out=b2_bf[:], in_=b2.rearrange("(m t) -> m t", t=H2_TILES))
        bp_rows = keep.tile([P, P], BF16)
        nc.gpsimd.memset(bp_rows[:], 0.0)
        nc.scalar.dma_start(out=bp_rows[0:NI_TILES, :], in_=bp.rearrange("(r n) i -> r (n i)", r=NI_TILES))

        eps = keep.tile([P, 1], F32)
        nc.vector.memset(eps[:], LN_EPS)
        first_rsqrt = keep.tile([P, 1], F32)
        nc.scalar.activation(out=first_rsqrt[:], in_=eps[:], func=ACT.Abs_reciprocal_sqrt)

        ident = keep.tile([P, P], F32)
        make_identity(nc, ident[:])
        in_capsule = keep.tile([P, CAPS_PER_TILE], F32)
        nc.vector.tensor_reduce(
            out=in_capsule[:],
            in_=ident[:].rearrange("p (n i) -> p n i", i=CAP_DIM),
            axis=mybir.AxisListType.X,
            op=ALU.add,
        )
        centre = keep.tile([P, P], F32)
        nc.vector.scalar_tensor_tensor(
            out=centre[:].rearrange("p (n i) -> p n i", i=CAP_DIM),
            in0=in_capsule[:].unsqueeze(2).to_broadcast([P, CAPS_PER_TILE, CAP_DIM]),
            scalar=-1.0 / CAP_DIM,
            in1=ident[:].rearrange("p (n i) -> p n i", i=CAP_DIM),
            op0=ALU.mult,
            op1=ALU.add,
        )

        w2_grouped = keep.tile([P, PASSES_1, H2, PACK], BF16, align_bytes=64)
        w2_codes = keep.tile([P, PASSES_1, H2], U32, align_bytes=64)
        w2_scales = keep.tile([P, PASSES_1, H2], U8, align_bytes=64)
        def regroup_w2(g):
            grouped = w2_grouped[:, g].rearrange("p (t m) j -> p t m j", t=H2_TILES)
            raw = w2_raw[:, g].rearrange("p j (m t) -> p t m j", t=H2_TILES)
            nc.vector.tensor_copy(out=grouped[:, :, 0:W2_VECTOR_UNITS, :], in_=raw[:, :, 0:W2_VECTOR_UNITS, :])
            nc.scalar.copy(out=grouped[:, :, W2_VECTOR_UNITS:P, :], in_=raw[:, :, W2_VECTOR_UNITS:P, :])

        def quantise_w2(g):
            nc.vector.quantize_mx(
                out=w2_codes[:, g, :].bitcast(FP8X4),
                scales=w2_scales[:, g, :],
                in_=w2_grouped[:, g].rearrange("p c j -> p (c j)"),
            )

        wp_grouped = keep.tile([P, CAPS, CAP_DIM, PACK], BF16, align_bytes=64)
        wp_codes = keep.tile([P, NI], U32, align_bytes=64)
        wp_scales = keep.tile([P, NI], U8, align_bytes=64)

        def regroup_wp():
            nc.vector.tensor_copy(out=wp_grouped[:], in_=wp_raw[:].rearrange("p n t i -> p n i t"))

        def quantise_wp():
            nc.vector.quantize_mx(
                out=wp_codes[:].bitcast(FP8X4),
                scales=wp_scales[:],
                in_=wp_grouped[:].rearrange("p n i t -> p (n i t)"),
            )

        h1_words = h1_raw[:].bitcast(F32)
        h1_grouped = keep.tile([P, ROW_TILES, PASSES_1, P, PACK], BF16, align_bytes=64)
        h1_grouped_words = h1_grouped[:].bitcast(F32)
        h1_codes = keep.tile([P, ROW_TILES, PASSES_1, P], U32, align_bytes=64)
        h1_scales = keep.tile([P, ROW_TILES, PASSES_1, P], U8, align_bytes=64)
        x_tiles = keep.tile([P, H2_TILES, B], BF16)
        x_grouped = keep.tile([P, B, PACK], BF16, align_bytes=64)
        x_codes = keep.tile([P, B], U32, align_bytes=64)
        x_scales = keep.tile([P, B], U8, align_bytes=64)
        u_t = keep.tile([P, NI_TILES, B], F32)
        out_tiles = out.rearrange("(j p) n i -> j p (n i)", p=P)

        turned_of = {}

        def turn_h1(j):
            turned = psum.tile([P, PASSES_1 * 2, P], F32, tag="plain")
            for g in range(PASSES_1):
                for u in range(2):
                    nc.tensor.transpose(
                        turned[:, 2 * g + u, :], h1_words[:, j, 256 * g + u : 256 * (g + 1) : 2], ident[:]
                    )
            turned_of[j] = turned

        def group_h1(j):
            nc.scalar.copy(out=h1_grouped_words[:, j], in_=turned_of[j][:].rearrange("p (g u) b -> p g b u", u=2))

        def quantise_h1(j):
            nc.vector.quantize_mx(
                out=h1_codes[:, j].rearrange("p g b -> p (g b)").bitcast(FP8X4),
                scales=h1_scales[:, j].rearrange("p g b -> p (g b)"),
                in_=h1_grouped[:, j].rearrange("p g b t -> p (g b t)"),
            )

        def first_product(j):
            rows = slice(j * P, (j + 1) * P)
            acc = psum_mx.tile([P, H2_TILES, P], F32, tag="mx")
            for t in range(H2_TILES):
                units = slice(t * P, (t + 1) * P)
                for g in range(PASSES_1):
                    nc.tensor.matmul_mx(
                        out=acc[:, t, :],
                        lhsT=w2_codes[:, g, units].bitcast(FP8X4),
                        lhsT_scale=w2_scales[:, g, units],
                        rhs=h1_codes[:, j, g, :].bitcast(FP8X4),
                        rhs_scale=h1_scales[:, j, g, :],
                        start=(g == 0),
                        stop=(g == PASSES_1 - 1),
                    )
            for t in range(H2_TILES):
                nc.scalar.activation(
                    out=x_tiles[:, t, rows], in_=acc[:, t, :], func=ACT.Relu, bias=b2_bf[:, t : t + 1], scale=1.0
                )

        def gather_x(j):
            rows = slice(j * P, (j + 1) * P)
            nc.vector.tensor_copy(
                out=x_grouped[:, rows, :].rearrange("p (c i) t -> p c t i", i=4),
                in_=x_tiles[:, :, rows].rearrange("p t (c i) -> p c t i", i=4),
            )

        def quantise_x(j):
            rows = slice(j * P, (j + 1) * P)
            nc.vector.quantize_mx(
                out=x_codes[:, rows].bitcast(FP8X4),
                scales=x_scales[:, rows],
                in_=x_grouped[:, rows, :].rearrange("p b t -> p (b t)"),
            )

        def second_product(j):
            rows = slice(j * P, (j + 1) * P)
            acc_t = psum_mx.tile([P, NI_TILES, P], F32, tag="mx")
            for r in range(NI_TILES):
                cols = slice(r * P, (r + 1) * P)
                nc.tensor.matmul_mx(
                    out=acc_t[:, r, :],
                    lhsT=wp_codes[:, cols].bitcast(FP8X4),
                    lhsT_scale=wp_scales[:, cols],
                    rhs=x_codes[:, rows].bitcast(FP8X4),
                    rhs_scale=x_scales[:, rows],
                    start=True,
                    stop=True,
                )
            for r in range(NI_TILES):
                nc.scalar.activation(
                    out=u_t[:, r, rows], in_=acc_t[:, r, :], func=ACT.Identity, bias=bp_col[:, r : r + 1], scale=1.0
                )

        centred_of, sum_sq_of, factor_of, scaled_of = {}, {}, {}, {}

        def capsule_parts(j):
            if j == ROW_TILES - 1:
                return (slice(0, CAPS // 2), slice(CAPS // 2, CAPS))
            return (slice(0, CAPS),)

        def centre_u(j):
            rows = slice(j * P, (j + 1) * P)
            centred = psum.tile([P, NI], F32, tag="plain")
            for r in range(NI_TILES):
                nc.tensor.matmul(
                    out=centred[:, r * P : (r + 1) * P], lhsT=u_t[:, r, rows], rhs=centre[:], start=True, stop=True
                )
            squares = work.tile([P, NI], F32)
            nc.scalar.activation(out=squares[:], in_=centred[:], func=ACT.Square)
            centred_of[j] = centred
            sum_sq_of[j] = squares

        def sum_squares(j):
            sum_sq = work.tile([P, CAPS], F32)
            nc.vector.tensor_reduce(
                out=sum_sq[:],
                in_=sum_sq_of[j][:].rearrange("p (n i) -> p n i", i=CAP_DIM),
                axis=mybir.AxisListType.X,
                op=ALU.add,
            )
            sum_sq_of[j] = sum_sq

        def make_factor(j):
            rstd = work.tile([P, CAPS], F32)
            nc.scalar.activation(
                out=rstd[:], in_=sum_sq_of[j][:], func=ACT.Abs_reciprocal_sqrt, bias=eps[:, 0:1], scale=1.0 / CAP_DIM
            )
            factor = work.tile([P, NI], F32)
            for caps in capsule_parts(j):
                cols = slice(caps.start * CAP_DIM, caps.stop * CAP_DIM)
                nc.gpsimd.tensor_tensor(
                    out=factor[:, cols].rearrange("p (n i) -> p n i", i=CAP_DIM),
                    in0=gain[:, cols].rearrange("p (n i) -> p n i", i=CAP_DIM),
                    in1=rstd[:, caps].unsqueeze(2).to_broadcast([P, caps.stop - caps.start, CAP_DIM]),
                    op=ALU.mult,
                )
            factor_of[j] = factor

        def scale_rows(j):
            scaled = work.tile([P, NI], F32)
            for caps in capsule_parts(j):
                cols = slice(caps.start * CAP_DIM, caps.stop * CAP_DIM)
                nc.vector.tensor_tensor(
                    out=scaled[:, cols], in0=centred_of[j][:, cols], in1=factor_of[j][:, cols], op=ALU.mult
                )
            scaled_of[j] = scaled

        def shift_and_store(j):
            result = work.tile([P, NI], F32)
            for caps in capsule_parts(j):
                cols = slice(caps.start * CAP_DIM, caps.stop * CAP_DIM)
                nc.vector.tensor_tensor(out=result[:, cols], in0=scaled_of[j][:, cols], in1=shift[:, cols], op=ALU.add)
                nc.sync.dma_start(out=out_tiles[j][:, cols], in_=result[:, cols])

        bp_rows_f = keep.tile([P, P], F32)
        bp_col = keep.tile([P, NI_TILES], F32)

        shift = psum_shift.tile([P, NI], F32)

        def turn_bp():
            nc.gpsimd.tensor_copy(out=bp_rows_f[:], in_=bp_rows[:])
            bp_ps = psum.tile([P, P], F32, tag="plain")
            nc.tensor.transpose(bp_ps[:], bp_rows_f[:], ident[:])
            nc.scalar.copy(out=bp_col[:], in_=bp_ps[:, 0:NI_TILES])

        def spread_shift():
            nc.tensor.matmul(out=shift[:], lhsT=ones[:], rhs=shift_row[:], start=True, stop=True)

        with tc.manual_schedule(engines={mybir.EngineType.PE, mybir.EngineType.Activation, mybir.EngineType.DVE}):
            regroup_w2(0)
            turn_h1(0)
            group_h1(0)
            regroup_w2(1)
            quantise_w2(0)
            quantise_w2(1)
            for j in range(1, EARLY_TILES):
                turn_h1(j)
                group_h1(j)
                quantise_h1(j - 1)
            quantise_h1(EARLY_TILES - 1)
            for j in range(EARLY_TILES):
                first_product(j)
                if j == 2:
                    turn_bp()
                if j == 1:
                    regroup_wp()
                    gather_x(0)
                    quantise_wp()
                    quantise_x(0)
                if j >= 2:
                    gather_x(j - 1)
                if j >= 3:
                    quantise_x(j - 2)
            gather_x(EARLY_TILES - 1)
            quantise_x(EARLY_TILES - 2)
            quantise_x(EARLY_TILES - 1)
            every = range(ROW_TILES)
            late = range(EARLY_TILES, ROW_TILES)
            for step in range(ROW_TILES + 5):
                if step == 3:
                    spread_shift()
                for stage, lag, tiles in (
                    (centre_u, 2, every),
                    (make_factor, 3, every),
                    (first_product, -3, late),
                    (shift_and_store, 5, every),
                    (quantise_x, -1, late),
                    (gather_x, -2, late),
                    (scale_rows, 4, every),
                    (sum_squares, 2, every),
                    (quantise_h1, -5, late),
                    (turn_h1, -6, late),
                    (second_product, 0, every),
                    (group_h1, -6, late),
                ):
                    if step - lag in tiles:
                        stage(step - lag)
